import numpy as np
import ml_dtypes

BF16 = ml_dtypes.bfloat16


def bf(x):
    return np.asarray(x, np.float32).astype(BF16)


def f32(x):
    return np.asarray(x, np.float32)


def f64(x):
    return np.asarray(x).astype(np.float64)


def striped(idx):
    return np.tile(idx.reshape(-1, 16).T, (8, 1))


H, D, F, C, S, N = 2, 128, 128, 512, 2048, 1024


def setup_inputs():
    bound = np.sqrt(6.0 / D)
    return {"base": f32(np.random.uniform(0.0, 4.0 / F, (C, S))), "keys": bf(np.random.standard_normal((H * D, N))), "wk": bf(np.random.uniform(-bound, bound, (H * D, F))), "offs": striped(np.random.permutation(S)[:N])}


def reference(base, keys, wk, offs):
    idx = offs[:16].T.reshape(-1)
    o = np.einsum("hdf,hdn->hfn", f64(wk).reshape(H, D, F), f64(keys).reshape(H, D, N))
    ep = np.exp(o)
    en = np.exp(-o)
    rp = 1.0 / ep.sum(axis=1, keepdims=True)
    rn = 1.0 / en.sum(axis=1, keepdims=True)
    phi = np.concatenate([ep * rp, en * rn], axis=1)
    out = f64(base).copy()
    out[:, idx] = phi.reshape(C, N)
    return out

@@ -1,0 +1,64 @@
+import concourse.mybir as mybir
+
+BF16, F32, U16 = mybir.dt.bfloat16, mybir.dt.float32, mybir.dt.uint16
+EXP = mybir.ActivationFunctionType.Exp
+MULT = mybir.AluOpType.mult
+
+H, D, F, S, N = 2, 128, 128, 2048, 1024
+CHUNK = 512
+N_CHUNKS = N // CHUNK
+OFFS_COLS = CHUNK // 16
+
+FLOPS = 2 * H * D * F * N + 2 * (2 * H) * F * N
+
+
+def tile_trainablehedgehog_kernel(tc, base, keys, wk, offs, out):
+    nc = tc.nc
+    with (
+        tc.tile_pool(name="held", bufs=1) as held,
+        tc.tile_pool(name="work", bufs=3) as work,
+        tc.psum_pool(name="proj", bufs=1) as proj,
+        tc.psum_pool(name="sums", bufs=2) as sums,
+    ):
+        offsets = held.tile([128, N // 16], U16, name="offsets")
+        nc.sync.dma_start(offsets[:], offs)
+
+        wk_sb, keys_sb = [], []
+        for h in range(H):
+            wk_sb.append(held.tile([D, F], BF16, name=f"wk{h}"))
+            nc.scalar.dma_start(wk_sb[h][:], wk[h * D : (h + 1) * D, :])
+            keys_sb.append(held.tile([D, N], BF16, name=f"keys{h}"))
+            nc.scalar.dma_start(keys_sb[h][:], keys[h * D : (h + 1) * D, :])
+        windows = []
+        for b in range(2 * H):
+            windows.append(held.tile([F, S], F32, name=f"window{b}"))
+            nc.sync.dma_start(windows[b][:], base[b * F : (b + 1) * F, :])
+
+        ones = held.tile([F, F], BF16, name="ones")
+        nc.vector.memset(ones[:], 1.0)
+
+        for h in range(H):
+            o = []
+            for c in range(N_CHUNKS):
+                o.append(proj.tile([F, CHUNK], F32, name=f"o{h}_{c}"))
+                nc.tensor.matmul(
+                    o[c][:], wk_sb[h][:], keys_sb[h][:, c * CHUNK : (c + 1) * CHUNK], start=True, stop=True
+                )
+            for half, sign in enumerate((1.0, -1.0)):
+                b = 2 * h + half
+                for c in range(N_CHUNKS):
+                    e16 = work.tile([F, CHUNK], BF16, name="e16")
+                    nc.scalar.activation(e16[:], o[c][:], EXP, scale=sign)
+                    e32 = work.tile([F, CHUNK], F32, name="e32")
+                    nc.scalar.activation(e32[:], o[c][:], EXP, scale=sign)
+                    total = sums.tile([F, CHUNK], F32, name="total")
+                    nc.tensor.matmul(total[:], ones[:], e16[:], start=True, stop=True)
+                    recip = work.tile([F, CHUNK], F32, name="recip")
+                    nc.vector.reciprocal(recip[:], total[:])
+                    nc.vector.tensor_tensor(
+                        windows[b][:].indirect(offsets[:, c * OFFS_COLS : (c + 1) * OFFS_COLS]),
+                        e32[:],
+                        recip[:],
+                        MULT,
+                    )
+                nc.sync.dma_start(out[b * F : (b + 1) * F, :], windows[b][:])

@@ -1,7 +1,7 @@
 import concourse.mybir as mybir
 
 BF16, F32, U16 = mybir.dt.bfloat16, mybir.dt.float32, mybir.dt.uint16
-EXP = mybir.ActivationFunctionType.Exp
+EXP, LN = mybir.ActivationFunctionType.Exp, mybir.ActivationFunctionType.Ln
 MULT = mybir.AluOpType.mult
 
 H, D, F, S, N = 2, 128, 128, 2048, 1024
@@ -53,8 +53,10 @@ def tile_trainablehedgehog_kernel(tc, base, keys, wk, offs, out):
                     nc.scalar.activation(e32[:], o[c][:], EXP, scale=sign)
                     total = sums.tile([F, CHUNK], F32, name="total")
                     nc.tensor.matmul(total[:], ones[:], e16[:], start=True, stop=True)
+                    log_total = work.tile([F, CHUNK], F32, name="log_total")
+                    nc.scalar.activation(log_total[:], total[:], LN)
                     recip = work.tile([F, CHUNK], F32, name="recip")
-                    nc.vector.reciprocal(recip[:], total[:])
+                    nc.scalar.activation(recip[:], log_total[:], EXP, scale=-1.0)
                     nc.vector.tensor_tensor(
                         windows[b][:].indirect(offsets[:, c * OFFS_COLS : (c + 1) * OFFS_COLS]),
                         e32[:],

@@ -1,12 +1,15 @@
 import concourse.mybir as mybir
+from concourse.masks import make_identity
 
 BF16, F32, U16 = mybir.dt.bfloat16, mybir.dt.float32, mybir.dt.uint16
-EXP, LN = mybir.ActivationFunctionType.Exp, mybir.ActivationFunctionType.Ln
+EXP = mybir.ActivationFunctionType.Exp
 MULT = mybir.AluOpType.mult
 
 H, D, F, S, N = 2, 128, 128, 2048, 1024
+P = 128
 CHUNK = 512
 N_CHUNKS = N // CHUNK
+GROUPS = CHUNK // P
 OFFS_COLS = CHUNK // 16
 
 FLOPS = 2 * H * D * F * N + 2 * (2 * H) * F * N
@@ -16,11 +19,12 @@ def tile_trainablehedgehog_kernel(tc, base, keys, wk, offs, out):
     nc = tc.nc
     with (
         tc.tile_pool(name="held", bufs=1) as held,
-        tc.tile_pool(name="work", bufs=3) as work,
+        tc.tile_pool(name="work", bufs=4) as work,
         tc.psum_pool(name="proj", bufs=1) as proj,
         tc.psum_pool(name="sums", bufs=2) as sums,
+        tc.psum_pool(name="spread", bufs=2) as spread,
     ):
-        offsets = held.tile([128, N // 16], U16, name="offsets")
+        offsets = held.tile([P, N // 16], U16, name="offsets")
         nc.sync.dma_start(offsets[:], offs)
 
         wk_sb, keys_sb = [], []
@@ -34,33 +38,57 @@ def tile_trainablehedgehog_kernel(tc, base, keys, wk, offs, out):
             windows.append(held.tile([F, S], F32, name=f"window{b}"))
             nc.sync.dma_start(windows[b][:], base[b * F : (b + 1) * F, :])
 
-        ones = held.tile([F, F], BF16, name="ones")
-        nc.vector.memset(ones[:], 1.0)
+        ones_col = held.tile([F, 1], BF16, name="ones_col")
+        nc.vector.memset(ones_col[:], 1.0)
+        identity = held.tile([P, P], F32, name="identity")
+        make_identity(nc, identity[:])
 
-        for h in range(H):
-            o = []
-            for c in range(N_CHUNKS):
-                o.append(proj.tile([F, CHUNK], F32, name=f"o{h}_{c}"))
+        o = {}
+        e32 = {}
+        totals = {}
+        recip = {}
+
+        def exponentials_and_sums(i, h, half, c):
+            if half == 0:
+                o[h, c] = proj.tile([F, CHUNK], F32, name=f"o{h}_{c}")
                 nc.tensor.matmul(
-                    o[c][:], wk_sb[h][:], keys_sb[h][:, c * CHUNK : (c + 1) * CHUNK], start=True, stop=True
+                    o[h, c][:], wk_sb[h][:], keys_sb[h][:, c * CHUNK : (c + 1) * CHUNK], start=True, stop=True
                 )
-            for half, sign in enumerate((1.0, -1.0)):
-                b = 2 * h + half
-                for c in range(N_CHUNKS):
-                    e16 = work.tile([F, CHUNK], BF16, name="e16")
-                    nc.scalar.activation(e16[:], o[c][:], EXP, scale=sign)
-                    e32 = work.tile([F, CHUNK], F32, name="e32")
-                    nc.scalar.activation(e32[:], o[c][:], EXP, scale=sign)
-                    total = sums.tile([F, CHUNK], F32, name="total")
-                    nc.tensor.matmul(total[:], ones[:], e16[:], start=True, stop=True)
-                    log_total = work.tile([F, CHUNK], F32, name="log_total")
-                    nc.scalar.activation(log_total[:], total[:], LN)
-                    recip = work.tile([F, CHUNK], F32, name="recip")
-                    nc.scalar.activation(recip[:], log_total[:], EXP, scale=-1.0)
-                    nc.vector.tensor_tensor(
-                        windows[b][:].indirect(offsets[:, c * OFFS_COLS : (c + 1) * OFFS_COLS]),
-                        e32[:],
-                        recip[:],
-                        MULT,
-                    )
+            sign = 1.0 - 2.0 * half
+            e16 = work.tile([F, CHUNK], BF16, name="e16")
+            nc.scalar.activation(e16[:], o[h, c][:], EXP, scale=sign)
+            e32[i] = work.tile([F, CHUNK], F32, name="e32")
+            nc.scalar.activation(e32[i][:], o[h, c][:], EXP, scale=sign)
+            totals[i] = sums.tile([P, GROUPS], F32, name="totals")
+            for g in range(GROUPS):
+                nc.tensor.matmul(
+                    totals[i][:, g : g + 1], e16[:, g * P : (g + 1) * P], ones_col[:], start=True, stop=True
+                )
+
+        def reciprocals(i):
+            recip_col = work.tile([P, GROUPS], F32, name="recip_col")
+            nc.vector.reciprocal(recip_col[:], totals[i][:])
+            recip_ps = spread.tile([F, CHUNK], F32, name="recip_ps")
+            for g in range(GROUPS):
+                nc.tensor.transpose(
+                    recip_ps[:, g * P : (g + 1) * P], recip_col[:, g : g + 1].to_broadcast([P, F]), identity[:]
+                )
+            recip[i] = work.tile([F, CHUNK], F32, name="recip")
+            nc.scalar.copy(recip[i][:], recip_ps[:])
+
+        def place(i, h, half, c):
+            b = 2 * h + half
+            nc.vector.tensor_tensor(
+                windows[b][:].indirect(offsets[:, c * OFFS_COLS : (c + 1) * OFFS_COLS]), e32[i][:], recip[i][:], MULT
+            )
+            if c == N_CHUNKS - 1:
                 nc.sync.dma_start(out[b * F : (b + 1) * F, :], windows[b][:])
+
+        chunks = [(h, half, c) for h in range(H) for half in range(2) for c in range(N_CHUNKS)]
+        for step in range(len(chunks) + 2):
+            if step < len(chunks):
+                exponentials_and_sums(step, *chunks[step])
+            if 1 <= step <= len(chunks):
+                reciprocals(step - 1)
+            if step >= 2:
+                place(step - 2, *chunks[step - 2])

@@ -27,16 +27,14 @@ def tile_trainablehedgehog_kernel(tc, base, keys, wk, offs, out):
         offsets = held.tile([P, N // 16], U16, name="offsets")
         nc.sync.dma_start(offsets[:], offs)
 
-        wk_sb, keys_sb = [], []
+        wk_sb = [held.tile([D, F], BF16, name=f"wk{h}") for h in range(H)]
+        keys_sb = [held.tile([D, N], BF16, name=f"keys{h}") for h in range(H)]
+        windows = [held.tile([F, S], F32, name=f"window{b}") for b in range(2 * H)]
         for h in range(H):
-            wk_sb.append(held.tile([D, F], BF16, name=f"wk{h}"))
-            nc.scalar.dma_start(wk_sb[h][:], wk[h * D : (h + 1) * D, :])
-            keys_sb.append(held.tile([D, N], BF16, name=f"keys{h}"))
-            nc.scalar.dma_start(keys_sb[h][:], keys[h * D : (h + 1) * D, :])
-        windows = []
-        for b in range(2 * H):
-            windows.append(held.tile([F, S], F32, name=f"window{b}"))
-            nc.sync.dma_start(windows[b][:], base[b * F : (b + 1) * F, :])
+            nc.sync.dma_start(wk_sb[h][:], wk[h * D : (h + 1) * D, :])
+            nc.sync.dma_start(keys_sb[h][:], keys[h * D : (h + 1) * D, :])
+            for b in (2 * h, 2 * h + 1):
+                nc.sync.dma_start(windows[b][:], base[b * F : (b + 1) * F, :])
 
         ones_col = held.tile([F, 1], BF16, name="ones_col")
         nc.vector.memset(ones_col[:], 1.0)

@@ -33,8 +33,8 @@ def tile_trainablehedgehog_kernel(tc, base, keys, wk, offs, out):
         for h in range(H):
             nc.sync.dma_start(wk_sb[h][:], wk[h * D : (h + 1) * D, :])
             nc.sync.dma_start(keys_sb[h][:], keys[h * D : (h + 1) * D, :])
-            for b in (2 * h, 2 * h + 1):
-                nc.sync.dma_start(windows[b][:], base[b * F : (b + 1) * F, :])
+        for b in range(2 * H):
+            nc.sync.dma_start(windows[b][:], base[b * F : (b + 1) * F, :])
 
         ones_col = held.tile([F, 1], BF16, name="ones_col")
         nc.vector.memset(ones_col[:], 1.0)
@@ -83,10 +83,7 @@ def tile_trainablehedgehog_kernel(tc, base, keys, wk, offs, out):
                 nc.sync.dma_start(out[b * F : (b + 1) * F, :], windows[b][:])
 
         chunks = [(h, half, c) for h in range(H) for half in range(2) for c in range(N_CHUNKS)]
-        for step in range(len(chunks) + 2):
-            if step < len(chunks):
-                exponentials_and_sums(step, *chunks[step])
-            if 1 <= step <= len(chunks):
-                reciprocals(step - 1)
-            if step >= 2:
-                place(step - 2, *chunks[step - 2])
+        for i, chunk in enumerate(chunks):
+            exponentials_and_sums(i, *chunk)
+            reciprocals(i)
+            place(i, *chunk)

@@ -7,10 +7,9 @@ MULT = mybir.AluOpType.mult
 
 H, D, F, S, N = 2, 128, 128, 2048, 1024
 P = 128
-CHUNK = 512
-N_CHUNKS = N // CHUNK
-GROUPS = CHUNK // P
-OFFS_COLS = CHUNK // 16
+BANK = 512
+
+UNITS = [(h, half, first, BANK) for h in range(H) for half in range(2) for first in range(0, N, BANK)]
 
 FLOPS = 2 * H * D * F * N + 2 * (2 * H) * F * N
 
@@ -19,71 +18,90 @@ def tile_trainablehedgehog_kernel(tc, base, keys, wk, offs, out):
     nc = tc.nc
     with (
         tc.tile_pool(name="held", bufs=1) as held,
-        tc.tile_pool(name="work", bufs=4) as work,
-        tc.psum_pool(name="proj", bufs=1) as proj,
+        tc.tile_pool(name="work", bufs=8) as work,
+        tc.psum_pool(name="proj", bufs=N // BANK) as proj,
         tc.psum_pool(name="sums", bufs=2) as sums,
-        tc.psum_pool(name="spread", bufs=2) as spread,
+        tc.psum_pool(name="spread", bufs=1) as spread,
+        tc.tile_pool(name="cols", bufs=1) as cols,
     ):
         offsets = held.tile([P, N // 16], U16, name="offsets")
-        nc.sync.dma_start(offsets[:], offs)
-
         wk_sb = [held.tile([D, F], BF16, name=f"wk{h}") for h in range(H)]
         keys_sb = [held.tile([D, N], BF16, name=f"keys{h}") for h in range(H)]
         windows = [held.tile([F, S], F32, name=f"window{b}") for b in range(2 * H)]
-        for h in range(H):
-            nc.sync.dma_start(wk_sb[h][:], wk[h * D : (h + 1) * D, :])
-            nc.sync.dma_start(keys_sb[h][:], keys[h * D : (h + 1) * D, :])
-        for b in range(2 * H):
+        nc.sync.dma_start(wk_sb[0][:], wk[0:D, :])
+        nc.sync.dma_start(keys_sb[0][:], keys[0:D, :])
+        nc.sync.dma_start(offsets[:], offs)
+        nc.sync.dma_start(windows[0][:], base[0:F, :])
+        nc.sync.dma_start(wk_sb[1][:], wk[D : 2 * D, :])
+        nc.sync.dma_start(keys_sb[1][:], keys[D : 2 * D, :])
+        for b in range(1, 2 * H):
             nc.sync.dma_start(windows[b][:], base[b * F : (b + 1) * F, :])
 
         ones_col = held.tile([F, 1], BF16, name="ones_col")
         nc.vector.memset(ones_col[:], 1.0)
         identity = held.tile([P, P], F32, name="identity")
-        make_identity(nc, identity[:])
+        nc.vector.memset(identity[:], 0.0)
+        make_identity(nc, identity[:], nomemset=True)
 
         o = {}
+        recip_ps = {}
         e32 = {}
-        totals = {}
         recip = {}
 
-        def exponentials_and_sums(i, h, half, c):
-            if half == 0:
-                o[h, c] = proj.tile([F, CHUNK], F32, name=f"o{h}_{c}")
+        def projections(h):
+            for k in range(N // BANK):
+                o[h, k] = proj.tile([F, BANK], F32, name="o")
                 nc.tensor.matmul(
-                    o[h, c][:], wk_sb[h][:], keys_sb[h][:, c * CHUNK : (c + 1) * CHUNK], start=True, stop=True
+                    o[h, k][:], wk_sb[h][:], keys_sb[h][:, k * BANK : (k + 1) * BANK], start=True, stop=True
                 )
-            sign = 1.0 - 2.0 * half
-            e16 = work.tile([F, CHUNK], BF16, name="e16")
-            nc.scalar.activation(e16[:], o[h, c][:], EXP, scale=sign)
-            e32[i] = work.tile([F, CHUNK], F32, name="e32")
-            nc.scalar.activation(e32[i][:], o[h, c][:], EXP, scale=sign)
-            totals[i] = sums.tile([P, GROUPS], F32, name="totals")
-            for g in range(GROUPS):
-                nc.tensor.matmul(
-                    totals[i][:, g : g + 1], e16[:, g * P : (g + 1) * P], ones_col[:], start=True, stop=True
-                )
+
+        def o_of(i):
+            h, half, first, width = UNITS[i]
+            return o[h, first // BANK][:, first % BANK : first % BANK + width]
 
         def reciprocals(i):
-            recip_col = work.tile([P, GROUPS], F32, name="recip_col")
-            nc.vector.reciprocal(recip_col[:], totals[i][:])
-            recip_ps = spread.tile([F, CHUNK], F32, name="recip_ps")
-            for g in range(GROUPS):
+            h, half, first, width = UNITS[i]
+            if half == 0 and first == 0:
+                projections(h)
+            e16 = work.tile([F, width], BF16, name="e16", tag=f"e16_{width}")
+            nc.scalar.activation(e16[:], o_of(i), EXP, scale=1.0 - 2.0 * half)
+            groups = width // P
+            totals = sums.tile([P, groups], F32, name="totals", tag="totals")
+            for g in range(groups):
+                nc.tensor.matmul(totals[:, g : g + 1], e16[:, g * P : (g + 1) * P], ones_col[:], start=True, stop=True)
+            recip_col = cols.tile([P, groups], F32, name="recip_col", tag="recip_col")
+            nc.vector.reciprocal(recip_col[:], totals[:])
+            recip_ps[i] = spread.tile([F, width], F32, name="recip_ps", tag="recip_ps")
+            for g in range(groups):
                 nc.tensor.transpose(
-                    recip_ps[:, g * P : (g + 1) * P], recip_col[:, g : g + 1].to_broadcast([P, F]), identity[:]
+                    recip_ps[i][:, g * P : (g + 1) * P], recip_col[:, g : g + 1].to_broadcast([P, F]), identity[:]
                 )
-            recip[i] = work.tile([F, CHUNK], F32, name="recip")
-            nc.scalar.copy(recip[i][:], recip_ps[:])
 
-        def place(i, h, half, c):
+        def factors(i):
+            h, half, first, width = UNITS[i]
+            e32[i] = work.tile([F, width], F32, name="e32", tag=f"e32_{width}")
+            nc.scalar.activation(e32[i][:], o_of(i), EXP, scale=1.0 - 2.0 * half)
+            recip[i] = work.tile([F, width], F32, name="recip", tag=f"recip_{width}")
+            if i == 0:
+                nc.vector.tensor_copy(recip[i][:], recip_ps[i][:])
+            else:
+                nc.scalar.copy(recip[i][:], recip_ps[i][:])
+
+        def place(i):
+            h, half, first, width = UNITS[i]
             b = 2 * h + half
             nc.vector.tensor_tensor(
-                windows[b][:].indirect(offsets[:, c * OFFS_COLS : (c + 1) * OFFS_COLS]), e32[i][:], recip[i][:], MULT
+                windows[b][:].indirect(offsets[:, first // 16 : (first + width) // 16]), e32[i][:], recip[i][:], MULT
             )
-            if c == N_CHUNKS - 1:
+            if first + width == N:
                 nc.sync.dma_start(out[b * F : (b + 1) * F, :], windows[b][:])
 
-        chunks = [(h, half, c) for h in range(H) for half in range(2) for c in range(N_CHUNKS)]
-        for i, chunk in enumerate(chunks):
-            exponentials_and_sums(i, *chunk)
-            reciprocals(i)
-            place(i, *chunk)
+        reciprocals(0)
+        reciprocals(1)
+        factors(0)
+        for i in range(len(UNITS)):
+            place(i)
+            if i + 2 < len(UNITS):
+                reciprocals(i + 2)
+            if i + 1 < len(UNITS):
+                factors(i + 1)

@@ -8,33 +8,41 @@ MULT = mybir.AluOpType.mult
 H, D, F, S, N = 2, 128, 128, 2048, 1024
 P = 128
 BANK = 512
-
-UNITS = [(h, half, first, BANK) for h in range(H) for half in range(2) for first in range(0, N, BANK)]
+BLOCKS = 2 * H
+UNITS = [(0, 0, 384), (0, 384, N)] + [(b, 0, N) for b in range(1, BLOCKS)]
 
 FLOPS = 2 * H * D * F * N + 2 * (2 * H) * F * N
+
+
+def runs(first, end):
+    return [(k, max(first, k * BANK), min(end, (k + 1) * BANK)) for k in range(first // BANK, (end - 1) // BANK + 1)]
 
 
 def tile_trainablehedgehog_kernel(tc, base, keys, wk, offs, out):
     nc = tc.nc
     with (
         tc.tile_pool(name="held", bufs=1) as held,
-        tc.tile_pool(name="work", bufs=8) as work,
+        tc.tile_pool(name="work", bufs=len(UNITS)) as work,
         tc.psum_pool(name="proj", bufs=N // BANK) as proj,
         tc.psum_pool(name="sums", bufs=2) as sums,
-        tc.psum_pool(name="spread", bufs=1) as spread,
-        tc.tile_pool(name="cols", bufs=1) as cols,
+        tc.psum_pool(name="spread", bufs=4) as spread,
     ):
         offsets = held.tile([P, N // 16], U16, name="offsets")
         wk_sb = [held.tile([D, F], BF16, name=f"wk{h}") for h in range(H)]
         keys_sb = [held.tile([D, N], BF16, name=f"keys{h}") for h in range(H)]
-        windows = [held.tile([F, S], F32, name=f"window{b}") for b in range(2 * H)]
-        nc.sync.dma_start(wk_sb[0][:], wk[0:D, :])
-        nc.sync.dma_start(keys_sb[0][:], keys[0:D, :])
+        windows = [held.tile([F, S], F32, name=f"window{b}") for b in range(BLOCKS)]
+        def load_head(h):
+            nc.sync.dma_start(wk_sb[h][:], wk[h * D : (h + 1) * D, :])
+            for k in range(N // BANK):
+                nc.sync.dma_start(
+                    keys_sb[h][:, k * BANK : (k + 1) * BANK], keys[h * D : (h + 1) * D, k * BANK : (k + 1) * BANK]
+                )
+
+        load_head(0)
         nc.sync.dma_start(offsets[:], offs)
         nc.sync.dma_start(windows[0][:], base[0:F, :])
-        nc.sync.dma_start(wk_sb[1][:], wk[D : 2 * D, :])
-        nc.sync.dma_start(keys_sb[1][:], keys[D : 2 * D, :])
-        for b in range(1, 2 * H):
+        load_head(1)
+        for b in range(1, BLOCKS):
             nc.sync.dma_start(windows[b][:], base[b * F : (b + 1) * F, :])
 
         ones_col = held.tile([F, 1], BF16, name="ones_col")
@@ -44,64 +52,84 @@ def tile_trainablehedgehog_kernel(tc, base, keys, wk, offs, out):
         make_identity(nc, identity[:], nomemset=True)
 
         o = {}
+        recip_col = {}
         recip_ps = {}
         e32 = {}
         recip = {}
 
-        def projections(h):
-            for k in range(N // BANK):
-                o[h, k] = proj.tile([F, BANK], F32, name="o")
-                nc.tensor.matmul(
-                    o[h, k][:], wk_sb[h][:], keys_sb[h][:, k * BANK : (k + 1) * BANK], start=True, stop=True
+        def exponentials(dest, u):
+            b, first, end = UNITS[u]
+            for k, lo, hi in runs(first, end):
+                nc.scalar.activation(
+                    dest[:, lo - first : hi - first], o[b // 2, k][:, lo - k * BANK : hi - k * BANK], EXP,
+                    scale=1.0 - 2.0 * (b % 2),
                 )
 
-        def o_of(i):
-            h, half, first, width = UNITS[i]
-            return o[h, first // BANK][:, first % BANK : first % BANK + width]
-
-        def reciprocals(i):
-            h, half, first, width = UNITS[i]
-            if half == 0 and first == 0:
-                projections(h)
-            e16 = work.tile([F, width], BF16, name="e16", tag=f"e16_{width}")
-            nc.scalar.activation(e16[:], o_of(i), EXP, scale=1.0 - 2.0 * half)
-            groups = width // P
-            totals = sums.tile([P, groups], F32, name="totals", tag="totals")
-            for g in range(groups):
+        def reciprocals(u):
+            b, first, end = UNITS[u]
+            if b % 2 == 0 and first == 0:
+                h = b // 2
+                for k in range(N // BANK):
+                    o[h, k] = proj.tile([F, BANK], F32, name="o")
+                    nc.tensor.matmul(
+                        o[h, k][:], wk_sb[h][:], keys_sb[h][:, k * BANK : (k + 1) * BANK], start=True, stop=True
+                    )
+            e16 = work.tile([F, end - first], BF16, name="e16", tag="e16")
+            exponentials(e16, u)
+            columns = (end - first) // P
+            totals = sums.tile([P, columns], F32, name="totals", tag="totals")
+            for g in range(columns):
                 nc.tensor.matmul(totals[:, g : g + 1], e16[:, g * P : (g + 1) * P], ones_col[:], start=True, stop=True)
-            recip_col = cols.tile([P, groups], F32, name="recip_col", tag="recip_col")
-            nc.vector.reciprocal(recip_col[:], totals[:])
-            recip_ps[i] = spread.tile([F, width], F32, name="recip_ps", tag="recip_ps")
-            for g in range(groups):
-                nc.tensor.transpose(
-                    recip_ps[i][:, g * P : (g + 1) * P], recip_col[:, g : g + 1].to_broadcast([P, F]), identity[:]
-                )
+            recip_col[u] = work.tile([P, columns], F32, name="recip_col", tag="recip_col")
+            nc.vector.reciprocal(recip_col[u][:], totals[:])
 
-        def factors(i):
-            h, half, first, width = UNITS[i]
-            e32[i] = work.tile([F, width], F32, name="e32", tag=f"e32_{width}")
-            nc.scalar.activation(e32[i][:], o_of(i), EXP, scale=1.0 - 2.0 * half)
-            recip[i] = work.tile([F, width], F32, name="recip", tag=f"recip_{width}")
-            if i == 0:
-                nc.vector.tensor_copy(recip[i][:], recip_ps[i][:])
-            else:
-                nc.scalar.copy(recip[i][:], recip_ps[i][:])
+        def spread_out(u):
+            b, first, end = UNITS[u]
+            for k, lo, hi in runs(first, end):
+                recip_ps[u, k] = spread.tile([F, hi - lo], F32, name="recip_ps", tag="recip_ps")
+                for t in range(lo, hi, P):
+                    column = recip_col[u][:, (t - first) // P : (t - first) // P + 1]
+                    nc.tensor.transpose(recip_ps[u, k][:, t - lo : t - lo + P], column.to_broadcast([P, F]), identity[:])
 
-        def place(i):
-            h, half, first, width = UNITS[i]
-            b = 2 * h + half
+        def first_factor(u):
+            b, first, end = UNITS[u]
+            e32[u] = work.tile([F, end - first], F32, name="e32", tag="e32")
+            exponentials(e32[u], u)
+
+        def second_factor(u):
+            b, first, end = UNITS[u]
+            recip[u] = work.tile([F, end - first], F32, name="recip", tag="recip")
+            for k, lo, hi in runs(first, end):
+                if u == 0:
+                    nc.vector.tensor_copy(recip[u][:, lo - first : hi - first], recip_ps[u, k][:])
+                else:
+                    nc.scalar.copy(recip[u][:, lo - first : hi - first], recip_ps[u, k][:])
+
+        def place(u):
+            b, first, end = UNITS[u]
             nc.vector.tensor_tensor(
-                windows[b][:].indirect(offsets[:, first // 16 : (first + width) // 16]), e32[i][:], recip[i][:], MULT
+                windows[b][:].indirect(offsets[:, first // 16 : end // 16]), e32[u][:], recip[u][:], MULT
             )
-            if first + width == N:
+            if end == N:
                 nc.sync.dma_start(out[b * F : (b + 1) * F, :], windows[b][:])
 
         reciprocals(0)
         reciprocals(1)
-        factors(0)
-        for i in range(len(UNITS)):
-            place(i)
-            if i + 2 < len(UNITS):
-                reciprocals(i + 2)
-            if i + 1 < len(UNITS):
-                factors(i + 1)
+        spread_out(0)
+        first_factor(0)
+        second_factor(0)
+        place(0)
+        spread_out(1)
+        first_factor(1)
+        first_factor(2)
+        reciprocals(2)
+        second_factor(1)
+        for u in range(1, len(UNITS)):
+            place(u)
+            if u + 2 < len(UNITS):
+                reciprocals(u + 2)
+            if u + 1 < len(UNITS):
+                spread_out(u + 1)
+                second_factor(u + 1)
+            if u + 2 < len(UNITS):
+                first_factor(u + 2)

@@ -9,13 +9,14 @@ H, D, F, S, N = 2, 128, 128, 2048, 1024
 P = 128
 BANK = 512
 BLOCKS = 2 * H
-UNITS = [(0, 0, 384), (0, 384, N)] + [(b, 0, N) for b in range(1, BLOCKS)]
+PIECES = [[(0, 256), (256, 640), (640, N)], [(0, BANK), (BANK, N)]]
+UNITS = [(0, lo, hi) for lo, hi in PIECES[0]] + [(b, 0, N) for b in range(1, BLOCKS)]
 
 FLOPS = 2 * H * D * F * N + 2 * (2 * H) * F * N
 
 
-def runs(first, end):
-    return [(k, max(first, k * BANK), min(end, (k + 1) * BANK)) for k in range(first // BANK, (end - 1) // BANK + 1)]
+def chunks(first, end):
+    return [(lo, min(lo + BANK, end)) for lo in range(first, end, BANK)]
 
 
 def tile_trainablehedgehog_kernel(tc, base, keys, wk, offs, out):
@@ -23,9 +24,9 @@ def tile_trainablehedgehog_kernel(tc, base, keys, wk, offs, out):
     with (
         tc.tile_pool(name="held", bufs=1) as held,
         tc.tile_pool(name="work", bufs=len(UNITS)) as work,
-        tc.psum_pool(name="proj", bufs=N // BANK) as proj,
-        tc.psum_pool(name="sums", bufs=2) as sums,
-        tc.psum_pool(name="spread", bufs=4) as spread,
+        tc.psum_pool(name="proj", bufs=sum(len(pieces) for pieces in PIECES)) as proj,
+        tc.psum_pool(name="turns", bufs=1) as turns,
+        tc.psum_pool(name="second", bufs=1) as second,
     ):
         offsets = held.tile([P, N // 16], U16, name="offsets")
         wk_sb = [held.tile([D, F], BF16, name=f"wk{h}") for h in range(H)]
@@ -33,17 +34,15 @@ def tile_trainablehedgehog_kernel(tc, base, keys, wk, offs, out):
         windows = [held.tile([F, S], F32, name=f"window{b}") for b in range(BLOCKS)]
         def load_head(h):
             nc.sync.dma_start(wk_sb[h][:], wk[h * D : (h + 1) * D, :])
-            for k in range(N // BANK):
-                nc.sync.dma_start(
-                    keys_sb[h][:, k * BANK : (k + 1) * BANK], keys[h * D : (h + 1) * D, k * BANK : (k + 1) * BANK]
-                )
+            for lo, hi in PIECES[h]:
+                nc.sync.dma_start(keys_sb[h][:, lo:hi], keys[h * D : (h + 1) * D, lo:hi])
 
         load_head(0)
         nc.sync.dma_start(offsets[:], offs)
-        nc.sync.dma_start(windows[0][:], base[0:F, :])
-        load_head(1)
-        for b in range(1, BLOCKS):
+        for b in range(BLOCKS):
             nc.sync.dma_start(windows[b][:], base[b * F : (b + 1) * F, :])
+            if b == 1:
+                load_head(1)
 
         ones_col = held.tile([F, 1], BF16, name="ones_col")
         nc.vector.memset(ones_col[:], 1.0)
@@ -59,37 +58,34 @@ def tile_trainablehedgehog_kernel(tc, base, keys, wk, offs, out):
 
         def exponentials(dest, u):
             b, first, end = UNITS[u]
-            for k, lo, hi in runs(first, end):
-                nc.scalar.activation(
-                    dest[:, lo - first : hi - first], o[b // 2, k][:, lo - k * BANK : hi - k * BANK], EXP,
-                    scale=1.0 - 2.0 * (b % 2),
-                )
+            for lo, hi in PIECES[b // 2]:
+                if first <= lo and hi <= end:
+                    nc.scalar.activation(dest[:, lo - first : hi - first], o[b // 2, lo][:], EXP, scale=1.0 - 2.0 * (b % 2))
 
         def reciprocals(u):
             b, first, end = UNITS[u]
-            if b % 2 == 0 and first == 0:
-                h = b // 2
-                for k in range(N // BANK):
-                    o[h, k] = proj.tile([F, BANK], F32, name="o")
-                    nc.tensor.matmul(
-                        o[h, k][:], wk_sb[h][:], keys_sb[h][:, k * BANK : (k + 1) * BANK], start=True, stop=True
-                    )
-            e16 = work.tile([F, end - first], BF16, name="e16", tag="e16")
+            h = b // 2
+            for lo, hi in PIECES[h]:
+                if b % 2 == 0 and first <= lo and hi <= end:
+                    o[h, lo] = proj.tile([F, hi - lo], F32, name="o")
+                    nc.tensor.matmul(o[h, lo][:], wk_sb[h][:], keys_sb[h][:, lo:hi], start=True, stop=True)
+            e16 = work.tile([F, end - first], BF16, name="e16", tag=f"ring{u % 2}", bufs=1)
             exponentials(e16, u)
             columns = (end - first) // P
-            totals = sums.tile([P, columns], F32, name="totals", tag="totals")
+            totals = turns.tile([P, columns], F32, name="totals", tag=f"turn{u % 2}")
             for g in range(columns):
                 nc.tensor.matmul(totals[:, g : g + 1], e16[:, g * P : (g + 1) * P], ones_col[:], start=True, stop=True)
-            recip_col[u] = work.tile([P, columns], F32, name="recip_col", tag="recip_col")
+            recip_col[u] = work.tile([P, columns], F32, name="recip_col", tag=f"ring{u % 2}", bufs=1)
             nc.vector.reciprocal(recip_col[u][:], totals[:])
 
         def spread_out(u):
             b, first, end = UNITS[u]
-            for k, lo, hi in runs(first, end):
-                recip_ps[u, k] = spread.tile([F, hi - lo], F32, name="recip_ps", tag="recip_ps")
+            for lo, hi in chunks(first, end):
+                pool, tag = (turns, f"turn{u % 2}") if lo == first else (second, "second")
+                recip_ps[u, lo] = pool.tile([F, hi - lo], F32, name="recip_ps", tag=tag)
                 for t in range(lo, hi, P):
                     column = recip_col[u][:, (t - first) // P : (t - first) // P + 1]
-                    nc.tensor.transpose(recip_ps[u, k][:, t - lo : t - lo + P], column.to_broadcast([P, F]), identity[:])
+                    nc.tensor.transpose(recip_ps[u, lo][:, t - lo : t - lo + P], column.to_broadcast([P, F]), identity[:])
 
         def first_factor(u):
             b, first, end = UNITS[u]
@@ -99,11 +95,11 @@ def tile_trainablehedgehog_kernel(tc, base, keys, wk, offs, out):
         def second_factor(u):
             b, first, end = UNITS[u]
             recip[u] = work.tile([F, end - first], F32, name="recip", tag="recip")
-            for k, lo, hi in runs(first, end):
+            for lo, hi in chunks(first, end):
                 if u == 0:
-                    nc.vector.tensor_copy(recip[u][:, lo - first : hi - first], recip_ps[u, k][:])
+                    nc.vector.tensor_copy(recip[u][:, lo - first : hi - first], recip_ps[u, lo][:])
                 else:
-                    nc.scalar.copy(recip[u][:, lo - first : hi - first], recip_ps[u, k][:])
+                    nc.scalar.copy(recip[u][:, lo - first : hi - first], recip_ps[u, lo][:])
 
         def place(u):
             b, first, end = UNITS[u]
@@ -118,18 +114,12 @@ def tile_trainablehedgehog_kernel(tc, base, keys, wk, offs, out):
         spread_out(0)
         first_factor(0)
         second_factor(0)
-        place(0)
-        spread_out(1)
         first_factor(1)
-        first_factor(2)
-        reciprocals(2)
-        second_factor(1)
-        for u in range(1, len(UNITS)):
+        for u in range(len(UNITS)):
             place(u)
             if u + 2 < len(UNITS):
                 reciprocals(u + 2)
+                first_factor(u + 2)
             if u + 1 < len(UNITS):
                 spread_out(u + 1)
                 second_factor(u + 1)
-            if u + 2 < len(UNITS):
-                first_factor(u + 2)

@@ -1,5 +1,4 @@
 import concourse.mybir as mybir
-from concourse.masks import make_identity
 
 BF16, F32, U16 = mybir.dt.bfloat16, mybir.dt.float32, mybir.dt.uint16
 EXP = mybir.ActivationFunctionType.Exp
@@ -8,9 +7,11 @@ MULT = mybir.AluOpType.mult
 H, D, F, S, N = 2, 128, 128, 2048, 1024
 P = 128
 BANK = 512
+SQUARE = 32
 BLOCKS = 2 * H
 PIECES = [[(0, 256), (256, 640), (640, N)], [(0, BANK), (BANK, N)]]
-UNITS = [(0, lo, hi) for lo, hi in PIECES[0]] + [(b, 0, N) for b in range(1, BLOCKS)]
+HEAD_START = PIECES[0][0][1]
+UNITS = [(0, 0, HEAD_START), (0, HEAD_START, N)] + [(b, 0, N) for b in range(1, BLOCKS)]
 
 FLOPS = 2 * H * D * F * N + 2 * (2 * H) * F * N
 
@@ -25,8 +26,8 @@ def tile_trainablehedgehog_kernel(tc, base, keys, wk, offs, out):
         tc.tile_pool(name="held", bufs=1) as held,
         tc.tile_pool(name="work", bufs=len(UNITS)) as work,
         tc.psum_pool(name="proj", bufs=sum(len(pieces) for pieces in PIECES)) as proj,
-        tc.psum_pool(name="turns", bufs=1) as turns,
-        tc.psum_pool(name="second", bufs=1) as second,
+        tc.psum_pool(name="sums", bufs=1) as sums,
+        tc.psum_pool(name="spread", bufs=2) as spread,
     ):
         offsets = held.tile([P, N // 16], U16, name="offsets")
         wk_sb = [held.tile([D, F], BF16, name=f"wk{h}") for h in range(H)]
@@ -39,16 +40,24 @@ def tile_trainablehedgehog_kernel(tc, base, keys, wk, offs, out):
 
         load_head(0)
         nc.sync.dma_start(offsets[:], offs)
-        for b in range(BLOCKS):
+        nc.sync.dma_start(windows[0][:], base[0:F, :])
+        load_head(1)
+        for b in range(1, BLOCKS):
             nc.sync.dma_start(windows[b][:], base[b * F : (b + 1) * F, :])
-            if b == 1:
-                load_head(1)
 
         ones_col = held.tile([F, 1], BF16, name="ones_col")
         nc.vector.memset(ones_col[:], 1.0)
+        ones = held.tile([P, SQUARE], F32, name="ones")
+        nc.vector.memset(ones[:], 1.0)
+        count = held.tile([P, SQUARE], F32, name="count", align_bytes=64)
+        nc.vector.tensor_tensor_scan(count[:], ones[:], ones[:], 0.0, MULT, mybir.AluOpType.add)
+        count_down = held.tile([P, SQUARE], F32, name="count_down", align_bytes=64)
+        nc.vector.transpose(count_down[:], count[:])
         identity = held.tile([P, P], F32, name="identity")
         nc.vector.memset(identity[:], 0.0)
-        make_identity(nc, identity[:], nomemset=True)
+        for q in range(0, P, SQUARE):
+            block = slice(q, q + SQUARE)
+            nc.vector.tensor_tensor(identity[block, block], count[block, :], count_down[block, :], mybir.AluOpType.is_equal)
 
         o = {}
         recip_col = {}
@@ -69,20 +78,19 @@ def tile_trainablehedgehog_kernel(tc, base, keys, wk, offs, out):
                 if b % 2 == 0 and first <= lo and hi <= end:
                     o[h, lo] = proj.tile([F, hi - lo], F32, name="o")
                     nc.tensor.matmul(o[h, lo][:], wk_sb[h][:], keys_sb[h][:, lo:hi], start=True, stop=True)
-            e16 = work.tile([F, end - first], BF16, name="e16", tag=f"ring{u % 2}", bufs=1)
+            e16 = work.tile([F, end - first], BF16, name="e16", tag="e16")
             exponentials(e16, u)
             columns = (end - first) // P
-            totals = turns.tile([P, columns], F32, name="totals", tag=f"turn{u % 2}")
+            totals = sums.tile([P, columns], F32, name="totals", tag="totals")
             for g in range(columns):
                 nc.tensor.matmul(totals[:, g : g + 1], e16[:, g * P : (g + 1) * P], ones_col[:], start=True, stop=True)
-            recip_col[u] = work.tile([P, columns], F32, name="recip_col", tag=f"ring{u % 2}", bufs=1)
+            recip_col[u] = work.tile([P, columns], F32, name="recip_col", tag="recip_col")
             nc.vector.reciprocal(recip_col[u][:], totals[:])
 
         def spread_out(u):
             b, first, end = UNITS[u]
             for lo, hi in chunks(first, end):
-                pool, tag = (turns, f"turn{u % 2}") if lo == first else (second, "second")
-                recip_ps[u, lo] = pool.tile([F, hi - lo], F32, name="recip_ps", tag=tag)
+                recip_ps[u, lo] = spread.tile([F, hi - lo], F32, name="recip_ps", tag="recip_ps")
                 for t in range(lo, hi, P):
                     column = recip_col[u][:, (t - first) // P : (t - first) // P + 1]
                     nc.tensor.transpose(recip_ps[u, lo][:, t - lo : t - lo + P], column.to_broadcast([P, F]), identity[:])
@@ -114,12 +122,12 @@ def tile_trainablehedgehog_kernel(tc, base, keys, wk, offs, out):
         spread_out(0)
         first_factor(0)
         second_factor(0)
-        first_factor(1)
         for u in range(len(UNITS)):
             place(u)
-            if u + 2 < len(UNITS):
-                reciprocals(u + 2)
-                first_factor(u + 2)
             if u + 1 < len(UNITS):
                 spread_out(u + 1)
+            if u + 2 < len(UNITS):
+                reciprocals(u + 2)
+            if u + 1 < len(UNITS):
+                first_factor(u + 1)
                 second_factor(u + 1)

@@ -65,21 +65,31 @@ def tile_trainablehedgehog_kernel(tc, base, keys, wk, offs, out):
         e32 = {}
         recip = {}
 
-        def exponentials(dest, u):
+        def pieces_of(u):
             b, first, end = UNITS[u]
-            for lo, hi in PIECES[b // 2]:
-                if first <= lo and hi <= end:
-                    nc.scalar.activation(dest[:, lo - first : hi - first], o[b // 2, lo][:], EXP, scale=1.0 - 2.0 * (b % 2))
+            return [(lo, hi) for lo, hi in PIECES[b // 2] if first <= lo and hi <= end]
+
+        def exponentials(dest, u, pieces):
+            b, first, end = UNITS[u]
+            for lo, hi in pieces:
+                nc.scalar.activation(dest[:, lo - first : hi - first], o[b // 2, lo][:], EXP, scale=1.0 - 2.0 * (b % 2))
 
         def reciprocals(u):
             b, first, end = UNITS[u]
             h = b // 2
-            for lo, hi in PIECES[h]:
-                if b % 2 == 0 and first <= lo and hi <= end:
+            if b % 2 == 0:
+                for lo, hi in pieces_of(u):
                     o[h, lo] = proj.tile([F, hi - lo], F32, name="o")
                     nc.tensor.matmul(o[h, lo][:], wk_sb[h][:], keys_sb[h][:, lo:hi], start=True, stop=True)
             e16 = work.tile([F, end - first], BF16, name="e16", tag="e16")
-            exponentials(e16, u)
+            e32[u] = work.tile([F, end - first], F32, name="e32", tag="e32")
+            if u == 1:
+                (lo, hi), rest = pieces_of(u)[0], pieces_of(u)[1:]
+                exponentials(e32[u], u, [(lo, hi)])
+                nc.vector.tensor_copy(e16[:, lo - first : hi - first], e32[u][:, lo - first : hi - first])
+            else:
+                rest = pieces_of(u)
+            exponentials(e16, u, rest)
             columns = (end - first) // P
             totals = sums.tile([P, columns], F32, name="totals", tag="totals")
             for g in range(columns):
@@ -96,9 +106,7 @@ def tile_trainablehedgehog_kernel(tc, base, keys, wk, offs, out):
                     nc.tensor.transpose(recip_ps[u, lo][:, t - lo : t - lo + P], column.to_broadcast([P, F]), identity[:])
 
         def first_factor(u):
-            b, first, end = UNITS[u]
-            e32[u] = work.tile([F, end - first], F32, name="e32", tag="e32")
-            exponentials(e32[u], u)
+            exponentials(e32[u], u, pieces_of(u)[1:] if u == 1 else pieces_of(u))
 
         def second_factor(u):
             b, first, end = UNITS[u]

@@ -77,6 +77,19 @@ def tile_trainablehedgehog_kernel(tc, base, keys, wk, offs, out):
         def reciprocals(u):
             b, first, end = UNITS[u]
             h = b // 2
+            columns = (end - first) // P
+            if u == 0:
+                o_turned = sums.tile([P, columns, F], F32, name="o_turned", tag="totals")
+                for g in range(columns):
+                    nc.tensor.matmul(o_turned[:, g, :], keys_sb[h][:, g * P : (g + 1) * P], wk_sb[h][:], start=True, stop=True)
+                e_turned = held.tile([P, columns, F], F32, name="e_turned")
+                totals = held.tile([P, columns], F32, name="totals0")
+                for g in range(columns):
+                    nc.scalar.activation(e_turned[:, g, :], o_turned[:, g, :], EXP, accum_out=totals[:, g : g + 1])
+                e32[u] = work.tile([F, end - first], F32, name="e32", tag="e32")
+                recip_col[u] = work.tile([P, columns], F32, name="recip_col", tag="recip_col")
+                nc.vector.reciprocal(recip_col[u][:], totals[:])
+                return
             if b % 2 == 0:
                 for lo, hi in pieces_of(u):
                     o[h, lo] = proj.tile([F, hi - lo], F32, name="o")
@@ -90,7 +103,6 @@ def tile_trainablehedgehog_kernel(tc, base, keys, wk, offs, out):
             else:
                 rest = pieces_of(u)
             exponentials(e16, u, rest)
-            columns = (end - first) // P
             totals = sums.tile([P, columns], F32, name="totals", tag="totals")
             for g in range(columns):
                 nc.tensor.matmul(totals[:, g : g + 1], e16[:, g * P : (g + 1) * P], ones_col[:], start=True, stop=True)
@@ -127,6 +139,8 @@ def tile_trainablehedgehog_kernel(tc, base, keys, wk, offs, out):
 
         reciprocals(0)
         reciprocals(1)
+        o[0, 0] = proj.tile([F, HEAD_START], F32, name="o")
+        nc.tensor.matmul(o[0, 0][:], wk_sb[0][:], keys_sb[0][:, 0:HEAD_START], start=True, stop=True)
         spread_out(0)
         first_factor(0)
         second_factor(0)

import concourse.mybir as mybir

BF16, F32, U16 = mybir.dt.bfloat16, mybir.dt.float32, mybir.dt.uint16
EXP = mybir.ActivationFunctionType.Exp
MULT = mybir.AluOpType.mult

H, D, F, S, N = 2, 128, 128, 2048, 1024
P = 128
BANK = 512
SQUARE = 32
BLOCKS = 2 * H
PIECES = [[(0, 256), (256, 640), (640, N)], [(0, BANK), (BANK, N)]]
HEAD_START = PIECES[0][0][1]
UNITS = [(0, 0, HEAD_START), (0, HEAD_START, N)] + [(b, 0, N) for b in range(1, BLOCKS)]

FLOPS = 2 * H * D * F * N + 2 * (2 * H) * F * N


def chunks(first, end):
    return [(lo, min(lo + BANK, end)) for lo in range(first, end, BANK)]


def tile_trainablehedgehog_kernel(tc, base, keys, wk, offs, out):
    nc = tc.nc
    with (
        tc.tile_pool(name="held", bufs=1) as held,
        tc.tile_pool(name="work", bufs=len(UNITS)) as work,
        tc.psum_pool(name="proj", bufs=sum(len(pieces) for pieces in PIECES)) as proj,
        tc.psum_pool(name="sums", bufs=1) as sums,
        tc.psum_pool(name="spread", bufs=2) as spread,
    ):
        offsets = held.tile([P, N // 16], U16, name="offsets")
        wk_sb = [held.tile([D, F], BF16, name=f"wk{h}") for h in range(H)]
        keys_sb = [held.tile([D, N], BF16, name=f"keys{h}") for h in range(H)]
        windows = [held.tile([F, S], F32, name=f"window{b}") for b in range(BLOCKS)]
        def load_head(h):
            nc.sync.dma_start(wk_sb[h][:], wk[h * D : (h + 1) * D, :])
            for lo, hi in PIECES[h]:
                nc.sync.dma_start(keys_sb[h][:, lo:hi], keys[h * D : (h + 1) * D, lo:hi])

        load_head(0)
        nc.sync.dma_start(offsets[:], offs)
        nc.sync.dma_start(windows[0][:], base[0:F, :])
        load_head(1)
        for b in range(1, BLOCKS):
            nc.sync.dma_start(windows[b][:], base[b * F : (b + 1) * F, :])

        ones_col = held.tile([F, 1], BF16, name="ones_col")
        nc.vector.memset(ones_col[:], 1.0)
        ones = held.tile([P, SQUARE], F32, name="ones")
        nc.vector.memset(ones[:], 1.0)
        count = held.tile([P, SQUARE], F32, name="count", align_bytes=64)
        nc.vector.tensor_tensor_scan(count[:], ones[:], ones[:], 0.0, MULT, mybir.AluOpType.add)
        count_down = held.tile([P, SQUARE], F32, name="count_down", align_bytes=64)
        nc.vector.transpose(count_down[:], count[:])
        identity = held.tile([P, P], F32, name="identity")
        nc.vector.memset(identity[:], 0.0)
        for q in range(0, P, SQUARE):
            block = slice(q, q + SQUARE)
            nc.vector.tensor_tensor(identity[block, block], count[block, :], count_down[block, :], mybir.AluOpType.is_equal)

        o = {}
        recip_col = {}
        recip_ps = {}
        e32 = {}
        recip = {}

        def pieces_of(u):
            b, first, end = UNITS[u]
            return [(lo, hi) for lo, hi in PIECES[b // 2] if first <= lo and hi <= end]

        def exponentials(dest, u, pieces):
            b, first, end = UNITS[u]
            for lo, hi in pieces:
                nc.scalar.activation(dest[:, lo - first : hi - first], o[b // 2, lo][:], EXP, scale=1.0 - 2.0 * (b % 2))

        def reciprocals(u):
            b, first, end = UNITS[u]
            h = b // 2
            columns = (end - first) // P
            if u == 0:
                o_turned = sums.tile([P, columns, F], F32, name="o_turned", tag="totals")
                for g in range(columns):
                    nc.tensor.matmul(o_turned[:, g, :], keys_sb[h][:, g * P : (g + 1) * P], wk_sb[h][:], start=True, stop=True)
                e_turned = held.tile([P, columns, F], F32, name="e_turned")
                totals = held.tile([P, columns], F32, name="totals0")
                for g in range(columns):
                    nc.scalar.activation(e_turned[:, g, :], o_turned[:, g, :], EXP, accum_out=totals[:, g : g + 1])
                e32[u] = work.tile([F, end - first], F32, name="e32", tag="e32")
                recip_col[u] = work.tile([P, columns], F32, name="recip_col", tag="recip_col")
                nc.vector.reciprocal(recip_col[u][:], totals[:])
                return
            if b % 2 == 0:
                for lo, hi in pieces_of(u):
                    o[h, lo] = proj.tile([F, hi - lo], F32, name="o")
                    nc.tensor.matmul(o[h, lo][:], wk_sb[h][:], keys_sb[h][:, lo:hi], start=True, stop=True)
            e16 = work.tile([F, end - first], BF16, name="e16", tag="e16")
            e32[u] = work.tile([F, end - first], F32, name="e32", tag="e32")
            if u == 1:
                (lo, hi), rest = pieces_of(u)[0], pieces_of(u)[1:]
                exponentials(e32[u], u, [(lo, hi)])
                nc.vector.tensor_copy(e16[:, lo - first : hi - first], e32[u][:, lo - first : hi - first])
            else:
                rest = pieces_of(u)
            exponentials(e16, u, rest)
            totals = sums.tile([P, columns], F32, name="totals", tag="totals")
            for g in range(columns):
                nc.tensor.matmul(totals[:, g : g + 1], e16[:, g * P : (g + 1) * P], ones_col[:], start=True, stop=True)
            recip_col[u] = work.tile([P, columns], F32, name="recip_col", tag="recip_col")
            nc.vector.reciprocal(recip_col[u][:], totals[:])

        def spread_out(u):
            b, first, end = UNITS[u]
            for lo, hi in chunks(first, end):
                recip_ps[u, lo] = spread.tile([F, hi - lo], F32, name="recip_ps", tag="recip_ps")
                for t in range(lo, hi, P):
                    column = recip_col[u][:, (t - first) // P : (t - first) // P + 1]
                    nc.tensor.transpose(recip_ps[u, lo][:, t - lo : t - lo + P], column.to_broadcast([P, F]), identity[:])

        def first_factor(u):
            exponentials(e32[u], u, pieces_of(u)[1:] if u == 1 else pieces_of(u))

        def second_factor(u):
            b, first, end = UNITS[u]
            recip[u] = work.tile([F, end - first], F32, name="recip", tag="recip")
            for lo, hi in chunks(first, end):
                if u == 0:
                    nc.vector.tensor_copy(recip[u][:, lo - first : hi - first], recip_ps[u, lo][:])
                else:
                    nc.scalar.copy(recip[u][:, lo - first : hi - first], recip_ps[u, lo][:])

        def place(u):
            b, first, end = UNITS[u]
            nc.vector.tensor_tensor(
                windows[b][:].indirect(offsets[:, first // 16 : end // 16]), e32[u][:], recip[u][:], MULT
            )
            if end == N:
                nc.sync.dma_start(out[b * F : (b + 1) * F, :], windows[b][:])

        reciprocals(0)
        reciprocals(1)
        o[0, 0] = proj.tile([F, HEAD_START], F32, name="o")
        nc.tensor.matmul(o[0, 0][:], wk_sb[0][:], keys_sb[0][:, 0:HEAD_START], start=True, stop=True)
        spread_out(0)
        first_factor(0)
        second_factor(0)
        for u in range(len(UNITS)):
            place(u)
            if u + 1 < len(UNITS):
                spread_out(u + 1)
            if u + 2 < len(UNITS):
                reciprocals(u + 2)
            if u + 1 < len(UNITS):
                first_factor(u + 1)
                second_factor(u + 1)
